import numpy as np
import ml_dtypes


def mxq(x, axis, fmt="e4m3"):
    dtype, down = {"e4m3": (ml_dtypes.float8_e4m3fn, 7), "e5m2": (ml_dtypes.float8_e5m2, 14)}[fmt]
    v = np.moveaxis(np.asarray(x, np.float32).astype(ml_dtypes.bfloat16).astype(np.float64), axis, -1)
    blocks = v.reshape(v.shape[:-1] + (-1, 32))
    amax = np.abs(blocks).max(-1, keepdims=True)
    byte = np.maximum(np.where(amax > 0, np.frexp(amax)[1] - 1 + 127, 0) - down, 1)
    scale = np.exp2(byte - 127.0)
    codes = (blocks / scale).astype(np.float32).astype(dtype).astype(np.float64)
    return np.moveaxis((codes * scale).reshape(v.shape), -1, axis)


WIDE = False


def mx_kscale(k):
    if not WIDE:
        return np.ones(k)
    levels = np.array([20, -20, 10, -10, 0])
    a = np.random.permutation(np.resize(levels, k // 512 * 4)).reshape(k // 512, 4)
    idx = np.arange(k)
    return np.exp2(a[idx // 512, idx % 128 // 32])


BF16 = ml_dtypes.bfloat16


def bf(x):
    return np.asarray(x, np.float32).astype(BF16)


def f64(x):
    return np.asarray(x).astype(np.float64)


W, M, K, N = 4, 1024, 512, 1024


def setup_inputs():
    u = mx_kscale(N)
    x = np.random.standard_normal((W, M, K))
    weight = np.random.standard_normal((W, N, K)) / np.sqrt(W * K) / u[None, :, None]
    bias = np.random.standard_normal((W, M, N)) / np.sqrt(W)
    g = np.random.standard_normal((W, M // W, N)) * np.exp2(np.random.randint(-12, 1, (W, M // W, 1))) * 16.0 * u
    return {"x": bf(x), "weight": bf(weight), "bias": bf(bias), "grad_out": bf(g)}


def reference(x, weight, bias, grad_out):
    w, m, _ = x.shape
    n = weight.shape[1]
    gq = mxq(f64(grad_out).reshape(m, n), 1, "e5m2")
    wq = mxq(f64(weight), 1, "e4m3")
    return gq[None, :, :] @ wq

@@ -1,0 +1,157 @@
+from contextlib import ExitStack
+
+import concourse.mybir as mybir
+from concourse.masks import make_identity
+
+BF16 = mybir.dt.bfloat16
+F32 = mybir.dt.float32
+U32 = mybir.dt.uint32
+U8 = mybir.dt.uint8
+E4X4 = mybir.dt.float8_e4m3fn_x4
+E5X4 = mybir.dt.float8_e5m2_x4
+
+P = 128
+W, M, K, N = 4, 1024, 512, 1024
+MT = M // P
+NP = N // 512
+
+FLOPS = 2 * W * M * K * N
+BYTES = W * N * K * 2 + M * N * 2 + W * M * K * 4
+
+PIN = False
+V_TILES = {0: (1, 3), 1: (3, 7), 2: (3, 7), 3: (1, 3, 5, 7)}
+
+
+def tile_gemmrstritonpcie_t_kernel(tc, x, weight, bias, grad_out, out):
+    nc = tc.nc
+    with ExitStack() as ctx:
+        keep = ctx.enter_context(tc.tile_pool(name="keep", bufs=1))
+        psum = ctx.enter_context(tc.psum_pool(name="psum", bufs=8))
+        if PIN:
+            ctx.enter_context(tc.manual_schedule())
+
+        w_raw = [keep.tile([P, NP * 2048], BF16, name="w_raw%d" % r) for r in range(W)]
+        w_grp = [
+            [keep.tile([P, 2048], BF16, name="w_grp%d_%d" % (r, c), align_bytes=64) for c in range(NP)]
+            for r in range(W)
+        ]
+        w_codes = [keep.tile([P, NP * 512], U32, name="w_codes%d" % r, align_bytes=64) for r in range(W)]
+        w_scales = [keep.tile([P, NP * 512], U8, name="w_scales%d" % r, align_bytes=64) for r in range(W)]
+        g_raw = keep.tile([P, MT * N], BF16, name="g_raw")
+        g_grp = keep.tile([P, MT * N], BF16, name="g_grp", align_bytes=64)
+        g_codes = keep.tile([P, MT * NP * P], U32, name="g_codes", align_bytes=64)
+        g_scales = keep.tile([P, MT * NP * P], U8, name="g_scales", align_bytes=64)
+        o_sb = [
+            [keep.tile([P, 4 * K], F32, name="o_sb%d_%d" % (r, h)) for h in range(2)] for r in range(W)
+        ]
+        ident = keep.tile([P, P], F32, name="ident")
+
+        g_view = grad_out.rearrange("w (q i) n -> (w q) i n", i=MT)
+        w_view = [weight[r].rearrange("(c p j) k -> p c (j k)", c=NP, j=4) for r in range(W)]
+        o_view = [out[r].rearrange("(p i) k -> p i k", i=MT) for r in range(W)]
+
+        def load_w(r, c0, c1):
+            nc.sync.dma_start(
+                out=w_raw[r][:, c0 * 2048 : c1 * 2048].rearrange("p (c f) -> p c f", f=2048),
+                in_=w_view[r][:, c0:c1, :],
+            )
+
+        def load_g(i0, i1):
+            nc.sync.dma_start(
+                out=g_raw[:, i0 * N : i1 * N].rearrange("p (i n) -> p i n", n=N),
+                in_=g_view[:, i0:i1, :],
+            )
+
+        load_w(0, 0, 1)
+        load_w(0, 1, 2)
+        load_g(0, 2)
+        load_g(2, 4)
+        load_g(4, 8)
+        load_w(1, 0, 2)
+        load_w(2, 0, 2)
+        load_w(3, 0, 2)
+
+        make_identity(nc, ident[:])
+
+        g_raw32 = g_raw[:].bitcast(F32)
+        g_grp32 = g_grp[:].bitcast(F32)
+
+        def prep_w(r):
+            for c in range(NP):
+                nc.vector.tensor_copy(
+                    out=w_grp[r][c][:].rearrange("p (a b t) -> p a t b", b=4, t=4),
+                    in_=w_raw[r][:, c * 2048 : (c + 1) * 2048].rearrange("p (t a b) -> p a t b", t=4, b=4),
+                )
+            for c in range(NP):
+                nc.vector.quantize_mx(
+                    out=w_codes[r][:, c * 512 : (c + 1) * 512].bitcast(E4X4),
+                    scales=w_scales[r][:, c * 512 : (c + 1) * 512],
+                    in_=w_grp[r][c][:],
+                )
+
+        def flip_g(i):
+            bank = psum.tile([P, 512], F32, name="flip%d" % i, tag="bank")
+            for c in range(NP):
+                for u in range(2):
+                    base = 512 * i + 256 * c
+                    s = 2 * c + u
+                    nc.tensor.transpose(
+                        bank[:, s * P : (s + 1) * P],
+                        g_raw32[:, base + u : base + 256 : 2],
+                        ident[:],
+                    )
+            nc.scalar.copy(
+                out=g_grp32[:, 512 * i : 512 * (i + 1)].rearrange("p (c m u) -> p c m u", c=NP, u=2),
+                in_=bank[:].rearrange("p (c u m) -> p c m u", c=NP, u=2),
+            )
+
+        def quant_g(i0, i1):
+            nc.vector.quantize_mx(
+                out=g_codes[:, i0 * 256 : i1 * 256].bitcast(E5X4),
+                scales=g_scales[:, i0 * 256 : i1 * 256],
+                in_=g_grp[:, i0 * 1024 : i1 * 1024],
+            )
+
+        def mx(r, i):
+            acc = psum.tile([P, K], F32, name="acc%d_%d" % (r, i), tag="bank")
+            for c in range(NP):
+                s = (NP * i + c) * P
+                nc.tensor.matmul_mx(
+                    out=acc[:],
+                    lhsT=g_codes[:, s : s + P].bitcast(E5X4),
+                    lhsT_scale=g_scales[:, s : s + P],
+                    rhs=w_codes[r][:, c * 512 : (c + 1) * 512].bitcast(E4X4),
+                    rhs_scale=w_scales[r][:, c * 512 : (c + 1) * 512],
+                    start=(c == 0),
+                    stop=(c == NP - 1),
+                )
+            dst = o_sb[r][i // 4][:, (i % 4) * K : (i % 4 + 1) * K]
+            if i in V_TILES[r]:
+                nc.vector.tensor_copy(out=dst, in_=acc[:])
+            else:
+                nc.scalar.copy(out=dst, in_=acc[:])
+            if i % 4 == 3:
+                h = i // 4
+                nc.sync.dma_start(
+                    out=o_view[r][:, 4 * h : 4 * h + 4, :],
+                    in_=o_sb[r][h][:].rearrange("p (i k) -> p i k", k=K),
+                )
+
+        prep_w(0)
+        for i in range(4):
+            flip_g(i)
+        quant_g(0, 2)
+        quant_g(2, 4)
+        for i in range(4):
+            mx(0, i)
+        for i in range(4, 8):
+            flip_g(i)
+        quant_g(4, 8)
+        prep_w(1)
+        for i in range(4, 8):
+            mx(0, i)
+        for r in range(1, W):
+            if r + 1 < W:
+                prep_w(r + 1)
+            for i in range(MT):
+                mx(r, i)

@@ -18,8 +18,16 @@ NP = N // 512
 FLOPS = 2 * W * M * K * N
 BYTES = W * N * K * 2 + M * N * 2 + W * M * K * 4
 
-PIN = False
-V_TILES = {0: (1, 3), 1: (3, 7), 2: (3, 7), 3: (1, 3, 5, 7)}
+PIN = True
+V_TILES = ((2, 3), (2, 5), (2, 7), (3, 1), (3, 3), (3, 5), (3, 7))
+G_LOADS = ((0, 1), (1, 2), (2, 4), (4, 6), (6, 8))
+G_QUANTS = ((0, 1), (1, 2), (2, 4), (4, 8))
+
+
+def stores_of(r):
+    if r == W - 1:
+        return ((0, 2), (2, 4), (4, 6), (6, 7), (7, 8))
+    return ((0, 2), (2, 4), (4, 6), (6, 8))
 
 
 def tile_gemmrstritonpcie_t_kernel(tc, x, weight, bias, grad_out, out):
@@ -37,44 +45,55 @@ def tile_gemmrstritonpcie_t_kernel(tc, x, weight, bias, grad_out, out):
         ]
         w_codes = [keep.tile([P, NP * 512], U32, name="w_codes%d" % r, align_bytes=64) for r in range(W)]
         w_scales = [keep.tile([P, NP * 512], U8, name="w_scales%d" % r, align_bytes=64) for r in range(W)]
-        g_raw = keep.tile([P, MT * N], BF16, name="g_raw")
-        g_grp = keep.tile([P, MT * N], BF16, name="g_grp", align_bytes=64)
-        g_codes = keep.tile([P, MT * NP * P], U32, name="g_codes", align_bytes=64)
-        g_scales = keep.tile([P, MT * NP * P], U8, name="g_scales", align_bytes=64)
-        o_sb = [
-            [keep.tile([P, 4 * K], F32, name="o_sb%d_%d" % (r, h)) for h in range(2)] for r in range(W)
-        ]
+        g_raw = {}
+        for i0, i1 in G_LOADS:
+            t = keep.tile([P, (i1 - i0) * N], BF16, name="g_raw%d" % i0)
+            for i in range(i0, i1):
+                g_raw[i] = (t, i - i0)
+        g_grp, g_codes, g_scales = {}, {}, {}
+        for i0, i1 in G_QUANTS:
+            n_t = i1 - i0
+            tg = keep.tile([P, n_t * N], BF16, name="g_grp%d" % i0, align_bytes=64)
+            tcd = keep.tile([P, n_t * NP * P], U32, name="g_codes%d" % i0, align_bytes=64)
+            tsc = keep.tile([P, n_t * NP * P], U8, name="g_scales%d" % i0, align_bytes=64)
+            for i in range(i0, i1):
+                g_grp[i], g_codes[i], g_scales[i] = (tg, i - i0), (tcd, i - i0), (tsc, i - i0)
+        o_sb = {}
+        for r in range(W):
+            for i0, i1 in stores_of(r):
+                t = keep.tile([P, (i1 - i0) * K], F32, name="o_sb%d_%d" % (r, i0))
+                for i in range(i0, i1):
+                    o_sb[(r, i)] = (t, i - i0, i0, i1)
         ident = keep.tile([P, P], F32, name="ident")
 
         g_view = grad_out.rearrange("w (q i) n -> (w q) i n", i=MT)
-        w_view = [weight[r].rearrange("(c p j) k -> p c (j k)", c=NP, j=4) for r in range(W)]
+        w_view = [weight[r].rearrange("(s p e) k -> p s (e k)", s=2 * NP, e=2) for r in range(W)]
         o_view = [out[r].rearrange("(p i) k -> p i k", i=MT) for r in range(W)]
 
         def load_w(r, c0, c1):
             nc.sync.dma_start(
-                out=w_raw[r][:, c0 * 2048 : c1 * 2048].rearrange("p (c f) -> p c f", f=2048),
-                in_=w_view[r][:, c0:c1, :],
+                out=w_raw[r][:, c0 * 2048 : c1 * 2048].rearrange("p (s f) -> p s f", f=1024),
+                in_=w_view[r][:, 2 * c0 : 2 * c1, :],
             )
 
         def load_g(i0, i1):
             nc.sync.dma_start(
-                out=g_raw[:, i0 * N : i1 * N].rearrange("p (i n) -> p i n", n=N),
+                out=g_raw[i0][0][:].rearrange("p (i n) -> p i n", n=N),
                 in_=g_view[:, i0:i1, :],
             )
 
         load_w(0, 0, 1)
         load_w(0, 1, 2)
-        load_g(0, 2)
+        load_g(0, 1)
+        load_g(1, 2)
         load_g(2, 4)
-        load_g(4, 8)
         load_w(1, 0, 2)
+        load_g(4, 6)
+        load_g(6, 8)
         load_w(2, 0, 2)
         load_w(3, 0, 2)
 
         make_identity(nc, ident[:])
-
-        g_raw32 = g_raw[:].bitcast(F32)
-        g_grp32 = g_grp[:].bitcast(F32)
 
         def prep_w(r):
             for c in range(NP):
@@ -91,67 +110,74 @@ def tile_gemmrstritonpcie_t_kernel(tc, x, weight, bias, grad_out, out):
 
         def flip_g(i):
             bank = psum.tile([P, 512], F32, name="flip%d" % i, tag="bank")
-            for c in range(NP):
-                for u in range(2):
-                    base = 512 * i + 256 * c
-                    s = 2 * c + u
-                    nc.tensor.transpose(
-                        bank[:, s * P : (s + 1) * P],
-                        g_raw32[:, base + u : base + 256 : 2],
-                        ident[:],
-                    )
+            raw, j = g_raw[i]
+            raw32 = raw[:].bitcast(F32)
+            for s in range(2 * NP):
+                nc.tensor.transpose(
+                    bank[:, s * P : (s + 1) * P],
+                    raw32[:, 512 * j + s * P : 512 * j + (s + 1) * P],
+                    ident[:],
+                )
+            grp, j = g_grp[i]
             nc.scalar.copy(
-                out=g_grp32[:, 512 * i : 512 * (i + 1)].rearrange("p (c m u) -> p c m u", c=NP, u=2),
+                out=grp[:].bitcast(F32)[:, 512 * j : 512 * (j + 1)].rearrange("p (c m u) -> p c m u", c=NP, u=2),
                 in_=bank[:].rearrange("p (c u m) -> p c m u", c=NP, u=2),
             )
 
-        def quant_g(i0, i1):
+        def quant_g(i0):
             nc.vector.quantize_mx(
-                out=g_codes[:, i0 * 256 : i1 * 256].bitcast(E5X4),
-                scales=g_scales[:, i0 * 256 : i1 * 256],
-                in_=g_grp[:, i0 * 1024 : i1 * 1024],
+                out=g_codes[i0][0][:].bitcast(E5X4),
+                scales=g_scales[i0][0][:],
+                in_=g_grp[i0][0][:],
             )
 
         def mx(r, i):
             acc = psum.tile([P, K], F32, name="acc%d_%d" % (r, i), tag="bank")
+            codes, j = g_codes[i]
+            scales = g_scales[i][0]
             for c in range(NP):
-                s = (NP * i + c) * P
+                s = (NP * j + c) * P
                 nc.tensor.matmul_mx(
                     out=acc[:],
-                    lhsT=g_codes[:, s : s + P].bitcast(E5X4),
-                    lhsT_scale=g_scales[:, s : s + P],
+                    lhsT=codes[:, s : s + P].bitcast(E5X4),
+                    lhsT_scale=scales[:, s : s + P],
                     rhs=w_codes[r][:, c * 512 : (c + 1) * 512].bitcast(E4X4),
                     rhs_scale=w_scales[r][:, c * 512 : (c + 1) * 512],
                     start=(c == 0),
                     stop=(c == NP - 1),
                 )
-            dst = o_sb[r][i // 4][:, (i % 4) * K : (i % 4 + 1) * K]
-            if i in V_TILES[r]:
+            o_t, j, i0, i1 = o_sb[(r, i)]
+            dst = o_t[:, j * K : (j + 1) * K]
+            if (r, i) in V_TILES:
                 nc.vector.tensor_copy(out=dst, in_=acc[:])
             else:
                 nc.scalar.copy(out=dst, in_=acc[:])
-            if i % 4 == 3:
-                h = i // 4
+            if i == i1 - 1:
                 nc.sync.dma_start(
-                    out=o_view[r][:, 4 * h : 4 * h + 4, :],
-                    in_=o_sb[r][h][:].rearrange("p (i k) -> p i k", k=K),
+                    out=o_view[r][:, i0:i1, :],
+                    in_=o_t[:].rearrange("p (i k) -> p i k", k=K),
                 )
 
         prep_w(0)
         for i in range(4):
             flip_g(i)
-        quant_g(0, 2)
-        quant_g(2, 4)
+        quant_g(0)
+        quant_g(1)
+        quant_g(2)
         for i in range(4):
             mx(0, i)
-        for i in range(4, 8):
-            flip_g(i)
-        quant_g(4, 8)
         prep_w(1)
         for i in range(4, 8):
+            flip_g(i)
+        for i in range(4):
+            mx(1, i)
+        quant_g(4)
+        prep_w(2)
+        prep_w(3)
+        for i in range(4, 8):
             mx(0, i)
-        for r in range(1, W):
-            if r + 1 < W:
-                prep_w(r + 1)
+        for i in range(4, 8):
+            mx(1, i)
+        for r in range(2, W):
             for i in range(MT):
                 mx(r, i)

@@ -24,10 +24,17 @@ G_LOADS = ((0, 1), (1, 2), (2, 4), (4, 6), (6, 8))
 G_QUANTS = ((0, 1), (1, 2), (2, 4), (4, 8))
 
 
+V_FLIPS = (6, 7)
+STORES = (
+    ((0, 4), (4, 6), (6, 8)),
+    ((0, 2), (2, 4), (4, 6), (6, 8)),
+    ((0, 2), (2, 4), (4, 8)),
+    ((0, 4), (4, 6), (6, 8)),
+)
+
+
 def stores_of(r):
-    if r == W - 1:
-        return ((0, 2), (2, 4), (4, 6), (6, 7), (7, 8))
-    return ((0, 2), (2, 4), (4, 6), (6, 8))
+    return STORES[r]
 
 
 def tile_gemmrstritonpcie_t_kernel(tc, x, weight, bias, grad_out, out):
@@ -119,10 +126,12 @@ def tile_gemmrstritonpcie_t_kernel(tc, x, weight, bias, grad_out, out):
                     ident[:],
                 )
             grp, j = g_grp[i]
-            nc.scalar.copy(
-                out=grp[:].bitcast(F32)[:, 512 * j : 512 * (j + 1)].rearrange("p (c m u) -> p c m u", c=NP, u=2),
-                in_=bank[:].rearrange("p (c u m) -> p c m u", c=NP, u=2),
-            )
+            dst = grp[:].bitcast(F32)[:, 512 * j : 512 * (j + 1)].rearrange("p (c m u) -> p c m u", c=NP, u=2)
+            src = bank[:].rearrange("p (c u m) -> p c m u", c=NP, u=2)
+            if i in V_FLIPS:
+                nc.vector.tensor_copy(out=dst, in_=src)
+            else:
+                nc.scalar.copy(out=dst, in_=src)
 
         def quant_g(i0):
             nc.vector.quantize_mx(
@@ -169,9 +178,9 @@ def tile_gemmrstritonpcie_t_kernel(tc, x, weight, bias, grad_out, out):
         prep_w(1)
         for i in range(4, 8):
             flip_g(i)
+        quant_g(4)
         for i in range(4):
             mx(1, i)
-        quant_g(4)
         prep_w(2)
         prep_w(3)
         for i in range(4, 8):

@@ -18,7 +18,7 @@ NP = N // 512
 FLOPS = 2 * W * M * K * N
 BYTES = W * N * K * 2 + M * N * 2 + W * M * K * 4
 
-PIN = True
+PIN = False
 V_TILES = ((2, 3), (2, 5), (2, 7), (3, 1), (3, 3), (3, 5), (3, 7))
 G_LOADS = ((0, 1), (1, 2), (2, 4), (4, 6), (6, 8))
 G_QUANTS = ((0, 1), (1, 2), (2, 4), (4, 8))

@@ -18,7 +18,7 @@ NP = N // 512
 FLOPS = 2 * W * M * K * N
 BYTES = W * N * K * 2 + M * N * 2 + W * M * K * 4
 
-PIN = False
+PIN = True
 V_TILES = ((2, 3), (2, 5), (2, 7), (3, 1), (3, 3), (3, 5), (3, 7))
 G_LOADS = ((0, 1), (1, 2), (2, 4), (4, 6), (6, 8))
 G_QUANTS = ((0, 1), (1, 2), (2, 4), (4, 8))
@@ -74,13 +74,13 @@ def tile_gemmrstritonpcie_t_kernel(tc, x, weight, bias, grad_out, out):
         ident = keep.tile([P, P], F32, name="ident")
 
         g_view = grad_out.rearrange("w (q i) n -> (w q) i n", i=MT)
-        w_view = [weight[r].rearrange("(s p e) k -> p s (e k)", s=2 * NP, e=2) for r in range(W)]
+        w_view = [weight[r].rearrange("(c p t) k -> p c (t k)", c=NP, t=4) for r in range(W)]
         o_view = [out[r].rearrange("(p i) k -> p i k", i=MT) for r in range(W)]
 
         def load_w(r, c0, c1):
             nc.sync.dma_start(
-                out=w_raw[r][:, c0 * 2048 : c1 * 2048].rearrange("p (s f) -> p s f", f=1024),
-                in_=w_view[r][:, 2 * c0 : 2 * c1, :],
+                out=w_raw[r][:, c0 * 2048 : c1 * 2048].rearrange("p (c f) -> p c f", f=2048),
+                in_=w_view[r][:, c0:c1, :],
             )
 
         def load_g(i0, i1):
@@ -120,9 +120,11 @@ def tile_gemmrstritonpcie_t_kernel(tc, x, weight, bias, grad_out, out):
             raw, j = g_raw[i]
             raw32 = raw[:].bitcast(F32)
             for s in range(2 * NP):
+                c, u = s // 2, s % 2
+                base = 512 * j + 256 * c
                 nc.tensor.transpose(
                     bank[:, s * P : (s + 1) * P],
-                    raw32[:, 512 * j + s * P : 512 * j + (s + 1) * P],
+                    raw32[:, base + u : base + 256 : 2],
                     ident[:],
                 )
             grp, j = g_grp[i]

from contextlib import ExitStack

import concourse.mybir as mybir
from concourse.masks import make_identity

BF16 = mybir.dt.bfloat16
F32 = mybir.dt.float32
U32 = mybir.dt.uint32
U8 = mybir.dt.uint8
E4X4 = mybir.dt.float8_e4m3fn_x4
E5X4 = mybir.dt.float8_e5m2_x4

P = 128
W, M, K, N = 4, 1024, 512, 1024
MT = M // P
NP = N // 512

FLOPS = 2 * W * M * K * N
BYTES = W * N * K * 2 + M * N * 2 + W * M * K * 4

PIN = True
V_TILES = ((2, 3), (2, 5), (2, 7), (3, 1), (3, 3), (3, 5), (3, 7))
G_LOADS = ((0, 1), (1, 2), (2, 4), (4, 6), (6, 8))
G_QUANTS = ((0, 1), (1, 2), (2, 4), (4, 8))


V_FLIPS = (6, 7)
STORES = (
    ((0, 4), (4, 6), (6, 8)),
    ((0, 2), (2, 4), (4, 6), (6, 8)),
    ((0, 2), (2, 4), (4, 8)),
    ((0, 4), (4, 6), (6, 8)),
)


def stores_of(r):
    return STORES[r]


def tile_gemmrstritonpcie_t_kernel(tc, x, weight, bias, grad_out, out):
    nc = tc.nc
    with ExitStack() as ctx:
        keep = ctx.enter_context(tc.tile_pool(name="keep", bufs=1))
        psum = ctx.enter_context(tc.psum_pool(name="psum", bufs=8))
        if PIN:
            ctx.enter_context(tc.manual_schedule())

        w_raw = [keep.tile([P, NP * 2048], BF16, name="w_raw%d" % r) for r in range(W)]
        w_grp = [
            [keep.tile([P, 2048], BF16, name="w_grp%d_%d" % (r, c), align_bytes=64) for c in range(NP)]
            for r in range(W)
        ]
        w_codes = [keep.tile([P, NP * 512], U32, name="w_codes%d" % r, align_bytes=64) for r in range(W)]
        w_scales = [keep.tile([P, NP * 512], U8, name="w_scales%d" % r, align_bytes=64) for r in range(W)]
        g_raw = {}
        for i0, i1 in G_LOADS:
            t = keep.tile([P, (i1 - i0) * N], BF16, name="g_raw%d" % i0)
            for i in range(i0, i1):
                g_raw[i] = (t, i - i0)
        g_grp, g_codes, g_scales = {}, {}, {}
        for i0, i1 in G_QUANTS:
            n_t = i1 - i0
            tg = keep.tile([P, n_t * N], BF16, name="g_grp%d" % i0, align_bytes=64)
            tcd = keep.tile([P, n_t * NP * P], U32, name="g_codes%d" % i0, align_bytes=64)
            tsc = keep.tile([P, n_t * NP * P], U8, name="g_scales%d" % i0, align_bytes=64)
            for i in range(i0, i1):
                g_grp[i], g_codes[i], g_scales[i] = (tg, i - i0), (tcd, i - i0), (tsc, i - i0)
        o_sb = {}
        for r in range(W):
            for i0, i1 in stores_of(r):
                t = keep.tile([P, (i1 - i0) * K], F32, name="o_sb%d_%d" % (r, i0))
                for i in range(i0, i1):
                    o_sb[(r, i)] = (t, i - i0, i0, i1)
        ident = keep.tile([P, P], F32, name="ident")

        g_view = grad_out.rearrange("w (q i) n -> (w q) i n", i=MT)
        w_view = [weight[r].rearrange("(c p t) k -> p c (t k)", c=NP, t=4) for r in range(W)]
        o_view = [out[r].rearrange("(p i) k -> p i k", i=MT) for r in range(W)]

        def load_w(r, c0, c1):
            nc.sync.dma_start(
                out=w_raw[r][:, c0 * 2048 : c1 * 2048].rearrange("p (c f) -> p c f", f=2048),
                in_=w_view[r][:, c0:c1, :],
            )

        def load_g(i0, i1):
            nc.sync.dma_start(
                out=g_raw[i0][0][:].rearrange("p (i n) -> p i n", n=N),
                in_=g_view[:, i0:i1, :],
            )

        load_w(0, 0, 1)
        load_w(0, 1, 2)
        load_g(0, 1)
        load_g(1, 2)
        load_g(2, 4)
        load_w(1, 0, 2)
        load_g(4, 6)
        load_g(6, 8)
        load_w(2, 0, 2)
        load_w(3, 0, 2)

        make_identity(nc, ident[:])

        def prep_w(r):
            for c in range(NP):
                nc.vector.tensor_copy(
                    out=w_grp[r][c][:].rearrange("p (a b t) -> p a t b", b=4, t=4),
                    in_=w_raw[r][:, c * 2048 : (c + 1) * 2048].rearrange("p (t a b) -> p a t b", t=4, b=4),
                )
            for c in range(NP):
                nc.vector.quantize_mx(
                    out=w_codes[r][:, c * 512 : (c + 1) * 512].bitcast(E4X4),
                    scales=w_scales[r][:, c * 512 : (c + 1) * 512],
                    in_=w_grp[r][c][:],
                )

        def flip_g(i):
            bank = psum.tile([P, 512], F32, name="flip%d" % i, tag="bank")
            raw, j = g_raw[i]
            raw32 = raw[:].bitcast(F32)
            for s in range(2 * NP):
                c, u = s // 2, s % 2
                base = 512 * j + 256 * c
                nc.tensor.transpose(
                    bank[:, s * P : (s + 1) * P],
                    raw32[:, base + u : base + 256 : 2],
                    ident[:],
                )
            grp, j = g_grp[i]
            dst = grp[:].bitcast(F32)[:, 512 * j : 512 * (j + 1)].rearrange("p (c m u) -> p c m u", c=NP, u=2)
            src = bank[:].rearrange("p (c u m) -> p c m u", c=NP, u=2)
            if i in V_FLIPS:
                nc.vector.tensor_copy(out=dst, in_=src)
            else:
                nc.scalar.copy(out=dst, in_=src)

        def quant_g(i0):
            nc.vector.quantize_mx(
                out=g_codes[i0][0][:].bitcast(E5X4),
                scales=g_scales[i0][0][:],
                in_=g_grp[i0][0][:],
            )

        def mx(r, i):
            acc = psum.tile([P, K], F32, name="acc%d_%d" % (r, i), tag="bank")
            codes, j = g_codes[i]
            scales = g_scales[i][0]
            for c in range(NP):
                s = (NP * j + c) * P
                nc.tensor.matmul_mx(
                    out=acc[:],
                    lhsT=codes[:, s : s + P].bitcast(E5X4),
                    lhsT_scale=scales[:, s : s + P],
                    rhs=w_codes[r][:, c * 512 : (c + 1) * 512].bitcast(E4X4),
                    rhs_scale=w_scales[r][:, c * 512 : (c + 1) * 512],
                    start=(c == 0),
                    stop=(c == NP - 1),
                )
            o_t, j, i0, i1 = o_sb[(r, i)]
            dst = o_t[:, j * K : (j + 1) * K]
            if (r, i) in V_TILES:
                nc.vector.tensor_copy(out=dst, in_=acc[:])
            else:
                nc.scalar.copy(out=dst, in_=acc[:])
            if i == i1 - 1:
                nc.sync.dma_start(
                    out=o_view[r][:, i0:i1, :],
                    in_=o_t[:].rearrange("p (i k) -> p i k", k=K),
                )

        prep_w(0)
        for i in range(4):
            flip_g(i)
        quant_g(0)
        quant_g(1)
        quant_g(2)
        for i in range(4):
            mx(0, i)
        prep_w(1)
        for i in range(4, 8):
            flip_g(i)
        quant_g(4)
        for i in range(4):
            mx(1, i)
        prep_w(2)
        prep_w(3)
        for i in range(4, 8):
            mx(0, i)
        for i in range(4, 8):
            mx(1, i)
        for r in range(2, W):
            for i in range(MT):
                mx(r, i)
